import numpy as np
import ml_dtypes


def mxq(x, axis, fmt="e4m3"):
    dtype, down = {"e4m3": (ml_dtypes.float8_e4m3fn, 7), "e5m2": (ml_dtypes.float8_e5m2, 14)}[fmt]
    v = np.moveaxis(np.asarray(x, np.float32).astype(ml_dtypes.bfloat16).astype(np.float64), axis, -1)
    blocks = v.reshape(v.shape[:-1] + (-1, 32))
    amax = np.abs(blocks).max(-1, keepdims=True)
    byte = np.maximum(np.where(amax > 0, np.frexp(amax)[1] - 1 + 127, 0) - down, 1)
    scale = np.exp2(byte - 127.0)
    codes = (blocks / scale).astype(np.float32).astype(dtype).astype(np.float64)
    return np.moveaxis((codes * scale).reshape(v.shape), -1, axis)


WIDE = False


def mx_kscale(k):
    if not WIDE:
        return np.ones(k)
    levels = np.array([10, -10, 5, -5, 0])
    a = np.random.permutation(np.resize(levels, k // 512 * 4)).reshape(k // 512, 4)
    idx = np.arange(k)
    return np.exp2(a[idx // 512, idx % 128 // 32])


BF16 = ml_dtypes.bfloat16


def bf(x):
    return np.asarray(x, np.float32).astype(BF16)


def f64(x):
    return np.asarray(x).astype(np.float64)


E2M1 = np.array([0.0, 0.5, 1.0, 1.5, 2.0, 3.0, 4.0, 6.0, -0.0, -0.5, -1.0, -1.5, -2.0, -3.0, -4.0, -6.0])


def pack_weight(w, fmt):
    k, n = w.shape
    w = f64(bf(w)).reshape(k // 32, 32, n)
    amax = np.abs(w).max(1)
    if fmt == "e4m3":
        byte = np.frexp(amax)[1] - 1 + 127 - 7
    else:
        mant, ex = np.frexp(amax / 6.0)
        byte = np.where(mant > 0.5, ex, ex - 1) + 127
    byte = np.clip(np.where(amax > 0, byte, 1), 1, 254)
    scaled = (w * np.exp2(127.0 - byte)[:, None, :]).reshape(k, n).astype(np.float32)
    by_word = np.ascontiguousarray(scaled.reshape(k // 512, 128, 4, n).transpose(0, 1, 3, 2))
    if fmt == "e4m3":
        words = by_word.astype(ml_dtypes.float8_e4m3fn).view(np.uint8)
    else:
        c = by_word.astype(ml_dtypes.float4_e2m1fn).view(np.uint8) & 0xF
        words = c[..., 0::2] | (c[..., 1::2] << 4)
    return np.ascontiguousarray(words), np.ascontiguousarray(byte.astype(np.uint8).reshape(k // 512, 16, n))


def unpack_weight(words, scales, fmt):
    g, p, n, _ = words.shape
    if fmt == "e4m3":
        vals = np.ascontiguousarray(words).view(ml_dtypes.float8_e4m3fn).astype(np.float64)
    else:
        nib = np.empty((g, p, n, 4), np.uint8)
        nib[..., 0::2] = words & 0xF
        nib[..., 1::2] = words >> 4
        vals = E2M1[nib]
    vals = vals * np.repeat(np.exp2(scales.astype(np.float64) - 127.0), 8, axis=1)[..., None]
    return vals.transpose(0, 1, 3, 2).reshape(g * 512, n)


B, H, L, E, QD = 4, 1, 128, 16384, 128


def setup_inputs():
    s = mx_kscale(E)
    x = bf(np.random.standard_normal((B, H, L, E)) * s)
    Wk_words, Wk_scales = pack_weight((np.random.standard_normal((QD, E)) * 0.3 / np.sqrt(E) / s).T, "e4m3")
    bk = bf(0.1 + 0.1 * np.random.standard_normal(QD))
    Wv_words, Wv_scales = pack_weight((np.random.standard_normal((QD, E)) * 0.3 / np.sqrt(E) / s).T, "e4m3")
    bv = bf(0.1 + 0.1 * np.random.standard_normal(QD))
    return {"x": x,
            "Wk_words": Wk_words,
            "Wk_scales": Wk_scales,
            "bk": bk,
            "Wv_words": Wv_words,
            "Wv_scales": Wv_scales,
            "bv": bv}


def reference(x, Wk_words, Wk_scales, bk, Wv_words, Wv_scales, bv):
    xq = mxq(f64(x), 3, "e4m3")
    K = (xq @ unpack_weight(Wk_words, Wk_scales, "e4m3")) + f64(bk)
    V = (xq @ unpack_weight(Wv_words, Wv_scales, "e4m3")) + f64(bv)
    return K * V

@@ -1,0 +1,188 @@
+from contextlib import ExitStack
+
+import concourse.mybir as mybir
+from concourse.masks import make_identity
+
+BF16 = mybir.dt.bfloat16
+F32 = mybir.dt.float32
+I32 = mybir.dt.int32
+U32 = mybir.dt.uint32
+U8 = mybir.dt.uint8
+FP8X4 = mybir.dt.float8_e4m3fn_x4
+
+P = 128
+ROW_TILES = 4
+ROWS = ROW_TILES * P
+E = 16384
+QD = 128
+K_PASS = 4 * P
+GROUPS = E // K_PASS
+PAIRS = K_PASS // 2
+CHUNK_GROUPS = 4
+CHUNKS = GROUPS // CHUNK_GROUPS
+PREFETCH = 3
+WV_PLANE_ROW = 4
+
+FLOPS = 2 * ROWS * E * 2 * QD
+
+
+def tile_parallelretention_pa_k_kernel(tc, x, Wk_words, Wk_scales, bk, Wv_words, Wv_scales, bv, out):
+    nc = tc.nc
+    x_tiles = x.rearrange("b h l e -> (b h) l e")
+    out_rows = out.rearrange("b h l n -> l (b h) n")
+
+    with ExitStack() as ctx:
+        const = ctx.enter_context(tc.tile_pool(name="const", bufs=1))
+        x_pool = ctx.enter_context(tc.tile_pool(name="x", bufs=(PREFETCH + 1) * ROW_TILES))
+        w_pool = ctx.enter_context(tc.tile_pool(name="w", bufs=CHUNKS))
+        grouped_pool = ctx.enter_context(tc.tile_pool(name="grouped", bufs=2))
+        mx_pool = ctx.enter_context(tc.tile_pool(name="mx", bufs=3))
+        banks = ctx.enter_context(tc.psum_pool(name="banks", bufs=6))
+        sums = ctx.enter_context(tc.psum_pool(name="sums", bufs=1))
+        ctx.enter_context(tc.manual_schedule())
+
+        raw = {}
+        wk_words = {}
+        wv_words = {}
+
+        def load_x(c):
+            for rt in range(ROW_TILES):
+                raw[(c, rt)] = x_pool.tile([P, CHUNK_GROUPS * K_PASS], BF16, name="raw")
+                nc.sync.dma_start(
+                    out=raw[(c, rt)][:],
+                    in_=x_tiles[rt, :, c * CHUNK_GROUPS * K_PASS : (c + 1) * CHUNK_GROUPS * K_PASS],
+                )
+
+        def load_weight_words(c):
+            for words, dram, name in ((wk_words, Wk_words, "wk"), (wv_words, Wv_words, "wv")):
+                words[c] = w_pool.tile([P, CHUNK_GROUPS, QD], U32, name=name, align_bytes=64)
+                nc.sync.dma_start(
+                    out=words[c][:].bitcast(I32),
+                    in_=dram[c * CHUNK_GROUPS : (c + 1) * CHUNK_GROUPS]
+                    .rearrange("g p n t -> p g (n t)")
+                    .bitcast(I32),
+                )
+
+        w_planes = const.tile([P, GROUPS, QD], U8, name="w_planes", align_bytes=64)
+        nc.vector.memset(w_planes[:].rearrange("p g n -> p (g n)").bitcast(I32), 0)
+        bias_rows = const.tile([P, P], BF16, name="bias_rows")
+        nc.vector.memset(bias_rows[:], 0.0)
+        nc.scalar.dma_start(out=bias_rows[0:1, :], in_=bk.unsqueeze(0))
+        nc.scalar.dma_start(out=bias_rows[1:2, :], in_=bv.unsqueeze(0))
+        ident_f32 = const.tile([P, P], F32, name="ident_f32")
+        make_identity(nc, ident_f32[:])
+        ident_bf16 = const.tile([P, P], BF16, name="ident_bf16")
+        make_identity(nc, ident_bf16[:])
+
+        load_x(0)
+        for first_row, dram in ((0, Wk_scales), (WV_PLANE_ROW, Wv_scales)):
+            by_row = dram.rearrange("g (quad r) n -> r quad g n", r=4)
+            for r in range(4):
+                nc.sync.dma_start(
+                    out=w_planes[first_row + r : P : 32].bitcast(I32),
+                    in_=by_row[r].bitcast(I32),
+                )
+        load_weight_words(0)
+        for c in range(1, PREFETCH):
+            load_x(c)
+            load_weight_words(c)
+
+        bias_ps = banks.tile([P, P], BF16, name="bias_ps", tag="bank")
+        nc.tensor.transpose(bias_ps[:], bias_rows[:], ident_bf16[:])
+        bias_cols = const.tile([P, 2], F32, name="bias_cols")
+        nc.scalar.activation(
+            out=bias_cols[:], in_=bias_ps[:, 0:2], func=mybir.ActivationFunctionType.Identity
+        )
+
+        k_sum = sums.tile([QD, ROWS], F32, name="k_sum")
+        v_sum = sums.tile([QD, ROWS], F32, name="v_sum")
+
+        grouped = {}
+        x_words = {}
+        x_planes = {}
+
+        def transpose_row_tile(c, rt):
+            pairs = raw[(c, rt)][:].bitcast(F32)
+            for two in range(CHUNK_GROUPS // 2):
+                bank = banks.tile([P, 2, 2, P], F32, name="bank")
+                for i in range(2):
+                    g = 2 * two + i
+                    for u in range(2):
+                        nc.tensor.transpose(
+                            bank[:, i, u, :], pairs[:, g * PAIRS + u : (g + 1) * PAIRS : 2], ident_f32[:]
+                        )
+                halves_together = bank[:].rearrange("p g u r -> p g r u")
+                target = grouped[c][:].bitcast(F32)[:, 2 * two : 2 * two + 2, rt * P : (rt + 1) * P, :]
+                if (2 * rt + two) % 4 == 3:
+                    nc.vector.tensor_copy(out=target, in_=halves_together)
+                else:
+                    nc.scalar.copy(out=target, in_=halves_together)
+
+        def quantise(c):
+            for g in range(CHUNK_GROUPS):
+                nc.vector.quantize_mx(
+                    out=x_words[c][:, g, :].bitcast(FP8X4),
+                    scales=x_planes[c][:, g, :],
+                    in_=grouped[c][:, g].rearrange("p r t -> p (r t)"),
+                )
+
+        def multiply(c, g):
+            group = c * CHUNK_GROUPS + g
+            for acc, words, first_row in ((k_sum, wk_words, 0), (v_sum, wv_words, WV_PLANE_ROW)):
+                nc.tensor.matmul_mx(
+                    out=acc[:],
+                    lhsT=words[c][:, g, :].bitcast(FP8X4),
+                    lhsT_scale=w_planes[first_row:P, group, :],
+                    rhs=x_words[c][:, g, :].bitcast(FP8X4),
+                    rhs_scale=x_planes[c][:, g, :],
+                    start=(group == 0),
+                    stop=(group == GROUPS - 1),
+                )
+
+        for c in range(CHUNKS + 1):
+            if c + PREFETCH < CHUNKS:
+                load_x(c + PREFETCH)
+                load_weight_words(c + PREFETCH)
+            if c < CHUNKS:
+                grouped[c] = grouped_pool.tile([P, CHUNK_GROUPS, ROWS, 4], BF16, name="grouped", align_bytes=64)
+                x_words[c] = mx_pool.tile([P, CHUNK_GROUPS, ROWS], U32, name="x_words", align_bytes=64)
+                x_planes[c] = mx_pool.tile([P, CHUNK_GROUPS, ROWS], U8, name="x_planes", align_bytes=64)
+            for run in range(2):
+                if c < CHUNKS:
+                    transpose_row_tile(c, 2 * run)
+                    transpose_row_tile(c, 2 * run + 1)
+                if c > 0:
+                    multiply(c - 1, 2 * run)
+                    multiply(c - 1, 2 * run + 1)
+            if c < CHUNKS:
+                quantise(c)
+
+        k_biased = const.tile([QD, ROWS], F32, name="k_biased")
+        product = const.tile([QD, ROWS], F32, name="product")
+        out_sb = const.tile([P, ROW_TILES, QD], F32, name="out_sb")
+        for half in range(2):
+            rows = slice(half * 2 * P, (half + 1) * 2 * P)
+            nc.scalar.activation(
+                out=k_biased[:, rows],
+                in_=k_sum[:, rows],
+                func=mybir.ActivationFunctionType.Identity,
+                bias=bias_cols[:, 0:1],
+            )
+            nc.vector.scalar_tensor_tensor(
+                out=product[:, rows],
+                in0=v_sum[:, rows],
+                scalar=bias_cols[:, 1:2],
+                in1=k_biased[:, rows],
+                op0=mybir.AluOpType.add,
+                op1=mybir.AluOpType.mult,
+            )
+        for half in range(2):
+            back = banks.tile([P, 2, QD], F32, name="back", tag="bank")
+            for i in range(2):
+                rt = 2 * half + i
+                nc.tensor.transpose(back[:, i, :], product[:, rt * P : (rt + 1) * P], ident_f32[:])
+            if half == 0:
+                nc.scalar.copy(out=out_sb[:, 0:2, :], in_=back[:])
+            else:
+                nc.vector.tensor_copy(out=out_sb[:, 2:4, :], in_=back[:])
+            nc.sync.dma_start(out=out_rows[:, 2 * half : 2 * half + 2, :], in_=out_sb[:, 2 * half : 2 * half + 2, :])

@@ -12,177 +12,151 @@ FP8X4 = mybir.dt.float8_e4m3fn_x4
 
 P = 128
 ROW_TILES = 4
-ROWS = ROW_TILES * P
 E = 16384
 QD = 128
 K_PASS = 4 * P
 GROUPS = E // K_PASS
-PAIRS = K_PASS // 2
-CHUNK_GROUPS = 4
-CHUNKS = GROUPS // CHUNK_GROUPS
+TILE_GROUPS = 4
+CHUNKS = GROUPS // TILE_GROUPS
+TILES = CHUNKS * ROW_TILES
 PREFETCH = 3
-WV_PLANE_ROW = 4
 
-FLOPS = 2 * ROWS * E * 2 * QD
+FLOPS = 2 * ROW_TILES * P * E * 2 * QD
 
 
 def tile_parallelretention_pa_k_kernel(tc, x, Wk_words, Wk_scales, bk, Wv_words, Wv_scales, bv, out):
     nc = tc.nc
     x_tiles = x.rearrange("b h l e -> (b h) l e")
-    out_rows = out.rearrange("b h l n -> l (b h) n")
+    out_tiles = out.rearrange("b h l n -> (b h) l n")
 
     with ExitStack() as ctx:
         const = ctx.enter_context(tc.tile_pool(name="const", bufs=1))
         x_pool = ctx.enter_context(tc.tile_pool(name="x", bufs=(PREFETCH + 1) * ROW_TILES))
         w_pool = ctx.enter_context(tc.tile_pool(name="w", bufs=CHUNKS))
-        grouped_pool = ctx.enter_context(tc.tile_pool(name="grouped", bufs=2))
-        mx_pool = ctx.enter_context(tc.tile_pool(name="mx", bufs=3))
-        banks = ctx.enter_context(tc.psum_pool(name="banks", bufs=6))
-        sums = ctx.enter_context(tc.psum_pool(name="sums", bufs=1))
+        stage = ctx.enter_context(tc.tile_pool(name="stage", bufs=3))
+        mx_pool = ctx.enter_context(tc.tile_pool(name="mx", bufs=4))
+        result = ctx.enter_context(tc.tile_pool(name="result", bufs=ROW_TILES))
+        banks = ctx.enter_context(tc.psum_pool(name="banks", bufs=4))
+        sums_pool = ctx.enter_context(tc.psum_pool(name="sums", bufs=1))
         ctx.enter_context(tc.manual_schedule())
 
         raw = {}
-        wk_words = {}
-        wv_words = {}
+        w_words = {}
 
         def load_x(c):
             for rt in range(ROW_TILES):
-                raw[(c, rt)] = x_pool.tile([P, CHUNK_GROUPS * K_PASS], BF16, name="raw")
+                t = c * ROW_TILES + rt
+                raw[t] = x_pool.tile([P, TILE_GROUPS * K_PASS], BF16, name="raw")
                 nc.sync.dma_start(
-                    out=raw[(c, rt)][:],
-                    in_=x_tiles[rt, :, c * CHUNK_GROUPS * K_PASS : (c + 1) * CHUNK_GROUPS * K_PASS],
+                    out=raw[t][:],
+                    in_=x_tiles[rt, :, c * TILE_GROUPS * K_PASS : (c + 1) * TILE_GROUPS * K_PASS],
                 )
 
         def load_weight_words(c):
-            for words, dram, name in ((wk_words, Wk_words, "wk"), (wv_words, Wv_words, "wv")):
-                words[c] = w_pool.tile([P, CHUNK_GROUPS, QD], U32, name=name, align_bytes=64)
+            w_words[c] = w_pool.tile([P, TILE_GROUPS, 2, QD], U32, name="w_words", align_bytes=64)
+            for j, dram in enumerate((Wk_words, Wv_words)):
                 nc.sync.dma_start(
-                    out=words[c][:].bitcast(I32),
-                    in_=dram[c * CHUNK_GROUPS : (c + 1) * CHUNK_GROUPS]
+                    out=w_words[c][:, :, j, :].bitcast(I32),
+                    in_=dram[c * TILE_GROUPS : (c + 1) * TILE_GROUPS]
                     .rearrange("g p n t -> p g (n t)")
                     .bitcast(I32),
                 )
 
-        w_planes = const.tile([P, GROUPS, QD], U8, name="w_planes", align_bytes=64)
-        nc.vector.memset(w_planes[:].rearrange("p g n -> p (g n)").bitcast(I32), 0)
-        bias_rows = const.tile([P, P], BF16, name="bias_rows")
+        bias_rows = const.tile([P, 2 * QD], BF16, name="bias_rows")
         nc.vector.memset(bias_rows[:], 0.0)
-        nc.scalar.dma_start(out=bias_rows[0:1, :], in_=bk.unsqueeze(0))
-        nc.scalar.dma_start(out=bias_rows[1:2, :], in_=bv.unsqueeze(0))
+        nc.scalar.dma_start(out=bias_rows[0:1, 0:QD], in_=bk.unsqueeze(0))
+        nc.scalar.dma_start(out=bias_rows[0:1, QD : 2 * QD], in_=bv.unsqueeze(0))
+        ones = const.tile([P, P], BF16, name="ones")
+        nc.vector.memset(ones[:], 1.0)
+        w_planes = const.tile([P, GROUPS, 2, QD], U8, name="w_planes", align_bytes=64)
+        nc.vector.memset(w_planes[:].rearrange("p g j n -> p (g j n)").bitcast(I32), 0)
         ident_f32 = const.tile([P, P], F32, name="ident_f32")
         make_identity(nc, ident_f32[:])
-        ident_bf16 = const.tile([P, P], BF16, name="ident_bf16")
-        make_identity(nc, ident_bf16[:])
 
         load_x(0)
-        for first_row, dram in ((0, Wk_scales), (WV_PLANE_ROW, Wv_scales)):
+        for j, dram in enumerate((Wk_scales, Wv_scales)):
             by_row = dram.rearrange("g (quad r) n -> r quad g n", r=4)
             for r in range(4):
-                nc.sync.dma_start(
-                    out=w_planes[first_row + r : P : 32].bitcast(I32),
-                    in_=by_row[r].bitcast(I32),
-                )
+                nc.sync.dma_start(out=w_planes[r:P:32, :, j, :].bitcast(I32), in_=by_row[r].bitcast(I32))
         load_weight_words(0)
         for c in range(1, PREFETCH):
-            load_x(c)
             load_weight_words(c)
+            load_x(c)
 
-        bias_ps = banks.tile([P, P], BF16, name="bias_ps", tag="bank")
-        nc.tensor.transpose(bias_ps[:], bias_rows[:], ident_bf16[:])
-        bias_cols = const.tile([P, 2], F32, name="bias_cols")
-        nc.scalar.activation(
-            out=bias_cols[:], in_=bias_ps[:, 0:2], func=mybir.ActivationFunctionType.Identity
-        )
+        bias_ps = banks.tile([P, 2 * QD], F32, name="bias_ps", tag="bank")
+        nc.tensor.matmul(out=bias_ps[:], lhsT=ones[:], rhs=bias_rows[:], start=True, stop=True)
+        bias_all = const.tile([P, 2 * QD], F32, name="bias_all")
+        nc.scalar.copy(out=bias_all[:], in_=bias_ps[:])
 
-        k_sum = sums.tile([QD, ROWS], F32, name="k_sum")
-        v_sum = sums.tile([QD, ROWS], F32, name="v_sum")
+        sums = [sums_pool.tile([P, 2 * QD], F32, name="sums%d" % rt) for rt in range(ROW_TILES)]
 
         grouped = {}
         x_words = {}
         x_planes = {}
 
-        def transpose_row_tile(c, rt):
-            pairs = raw[(c, rt)][:].bitcast(F32)
-            for two in range(CHUNK_GROUPS // 2):
+        def transpose_tile(t):
+            by_half = stage.tile([P, TILE_GROUPS, 2, 2 * P], BF16, name="by_half")
+            nc.vector.tensor_copy(
+                out=by_half[:].bitcast(F32),
+                in_=raw[t][:].bitcast(F32).rearrange("r (g p u) -> r g u p", g=TILE_GROUPS, u=2),
+            )
+            grouped[t] = stage.tile([P, TILE_GROUPS, P, 4], BF16, name="grouped", align_bytes=64)
+            for two in range(TILE_GROUPS // 2):
                 bank = banks.tile([P, 2, 2, P], F32, name="bank")
                 for i in range(2):
-                    g = 2 * two + i
                     for u in range(2):
                         nc.tensor.transpose(
-                            bank[:, i, u, :], pairs[:, g * PAIRS + u : (g + 1) * PAIRS : 2], ident_f32[:]
+                            bank[:, i, u, :], by_half[:].bitcast(F32)[:, 2 * two + i, u, :], ident_f32[:]
                         )
-                halves_together = bank[:].rearrange("p g u r -> p g r u")
-                target = grouped[c][:].bitcast(F32)[:, 2 * two : 2 * two + 2, rt * P : (rt + 1) * P, :]
-                if (2 * rt + two) % 4 == 3:
-                    nc.vector.tensor_copy(out=target, in_=halves_together)
-                else:
-                    nc.scalar.copy(out=target, in_=halves_together)
-
-        def quantise(c):
-            for g in range(CHUNK_GROUPS):
-                nc.vector.quantize_mx(
-                    out=x_words[c][:, g, :].bitcast(FP8X4),
-                    scales=x_planes[c][:, g, :],
-                    in_=grouped[c][:, g].rearrange("p r t -> p (r t)"),
+                nc.scalar.copy(
+                    out=grouped[t][:].bitcast(F32)[:, 2 * two : 2 * two + 2, :, :],
+                    in_=bank[:].rearrange("p g u r -> p g r u"),
                 )
 
-        def multiply(c, g):
-            group = c * CHUNK_GROUPS + g
-            for acc, words, first_row in ((k_sum, wk_words, 0), (v_sum, wv_words, WV_PLANE_ROW)):
+        def quantise(t):
+            x_words[t] = mx_pool.tile([P, TILE_GROUPS, P], U32, name="x_words", align_bytes=64)
+            x_planes[t] = mx_pool.tile([P, TILE_GROUPS, P], U8, name="x_planes", align_bytes=64)
+            nc.vector.quantize_mx(
+                out=x_words[t][:].rearrange("p g r -> p (g r)").bitcast(FP8X4),
+                scales=x_planes[t][:].rearrange("p g r -> p (g r)"),
+                in_=grouped[t][:].rearrange("p g r t -> p (g r t)"),
+            )
+
+        def multiply(t):
+            c, rt = divmod(t, ROW_TILES)
+            for g in range(TILE_GROUPS):
+                group = c * TILE_GROUPS + g
                 nc.tensor.matmul_mx(
-                    out=acc[:],
-                    lhsT=words[c][:, g, :].bitcast(FP8X4),
-                    lhsT_scale=w_planes[first_row:P, group, :],
-                    rhs=x_words[c][:, g, :].bitcast(FP8X4),
-                    rhs_scale=x_planes[c][:, g, :],
+                    out=sums[rt][:],
+                    lhsT=x_words[t][:, g, :].bitcast(FP8X4),
+                    lhsT_scale=x_planes[t][:, g, :],
+                    rhs=w_words[c][:, g].rearrange("p j n -> p (j n)").bitcast(FP8X4),
+                    rhs_scale=w_planes[:, group].rearrange("p j n -> p (j n)"),
                     start=(group == 0),
                     stop=(group == GROUPS - 1),
                 )
 
-        for c in range(CHUNKS + 1):
-            if c + PREFETCH < CHUNKS:
-                load_x(c + PREFETCH)
-                load_weight_words(c + PREFETCH)
-            if c < CHUNKS:
-                grouped[c] = grouped_pool.tile([P, CHUNK_GROUPS, ROWS, 4], BF16, name="grouped", align_bytes=64)
-                x_words[c] = mx_pool.tile([P, CHUNK_GROUPS, ROWS], U32, name="x_words", align_bytes=64)
-                x_planes[c] = mx_pool.tile([P, CHUNK_GROUPS, ROWS], U8, name="x_planes", align_bytes=64)
-            for run in range(2):
-                if c < CHUNKS:
-                    transpose_row_tile(c, 2 * run)
-                    transpose_row_tile(c, 2 * run + 1)
-                if c > 0:
-                    multiply(c - 1, 2 * run)
-                    multiply(c - 1, 2 * run + 1)
-            if c < CHUNKS:
-                quantise(c)
+        def finish(rt):
+            biased = result.tile([P, 2 * QD], F32, name="biased")
+            nc.vector.tensor_add(out=biased[:], in0=sums[rt][:], in1=bias_all[:])
+            product = result.tile([P, QD], F32, name="product")
+            nc.vector.tensor_mul(out=product[:], in0=biased[:, 0:QD], in1=biased[:, QD : 2 * QD])
+            nc.sync.dma_start(out=out_tiles[rt], in_=product[:])
 
-        k_biased = const.tile([QD, ROWS], F32, name="k_biased")
-        product = const.tile([QD, ROWS], F32, name="product")
-        out_sb = const.tile([P, ROW_TILES, QD], F32, name="out_sb")
-        for half in range(2):
-            rows = slice(half * 2 * P, (half + 1) * 2 * P)
-            nc.scalar.activation(
-                out=k_biased[:, rows],
-                in_=k_sum[:, rows],
-                func=mybir.ActivationFunctionType.Identity,
-                bias=bias_cols[:, 0:1],
-            )
-            nc.vector.scalar_tensor_tensor(
-                out=product[:, rows],
-                in0=v_sum[:, rows],
-                scalar=bias_cols[:, 1:2],
-                in1=k_biased[:, rows],
-                op0=mybir.AluOpType.add,
-                op1=mybir.AluOpType.mult,
-            )
-        for half in range(2):
-            back = banks.tile([P, 2, QD], F32, name="back", tag="bank")
-            for i in range(2):
-                rt = 2 * half + i
-                nc.tensor.transpose(back[:, i, :], product[:, rt * P : (rt + 1) * P], ident_f32[:])
-            if half == 0:
-                nc.scalar.copy(out=out_sb[:, 0:2, :], in_=back[:])
-            else:
-                nc.vector.tensor_copy(out=out_sb[:, 2:4, :], in_=back[:])
-            nc.sync.dma_start(out=out_rows[:, 2 * half : 2 * half + 2, :], in_=out_sb[:, 2 * half : 2 * half + 2, :])
+        for t in range(TILES):
+            c, rt = divmod(t, ROW_TILES)
+            if rt == 0 and c + PREFETCH < CHUNKS:
+                load_weight_words(c + PREFETCH)
+                load_x(c + PREFETCH)
+            transpose_tile(t)
+            if t >= 1:
+                quantise(t - 1)
+            if t % 2 == 1:
+                if t >= 2:
+                    multiply(t - 2)
+                multiply(t - 1)
+        finish(0)
+        quantise(TILES - 1)
+        multiply(TILES - 1)
+        for rt in range(1, ROW_TILES):
+            finish(rt)

@@ -19,7 +19,7 @@ GROUPS = E // K_PASS
 TILE_GROUPS = 4
 CHUNKS = GROUPS // TILE_GROUPS
 TILES = CHUNKS * ROW_TILES
-PREFETCH = 3
+PREFETCH = 12
 
 FLOPS = 2 * ROW_TILES * P * E * 2 * QD
 
@@ -31,7 +31,7 @@ def tile_parallelretention_pa_k_kernel(tc, x, Wk_words, Wk_scales, bk, Wv_words,
 
     with ExitStack() as ctx:
         const = ctx.enter_context(tc.tile_pool(name="const", bufs=1))
-        x_pool = ctx.enter_context(tc.tile_pool(name="x", bufs=(PREFETCH + 1) * ROW_TILES))
+        x_pool = ctx.enter_context(tc.tile_pool(name="x", bufs=PREFETCH + 1))
         w_pool = ctx.enter_context(tc.tile_pool(name="w", bufs=CHUNKS))
         stage = ctx.enter_context(tc.tile_pool(name="stage", bufs=3))
         mx_pool = ctx.enter_context(tc.tile_pool(name="mx", bufs=4))
@@ -43,14 +43,13 @@ def tile_parallelretention_pa_k_kernel(tc, x, Wk_words, Wk_scales, bk, Wv_words,
         raw = {}
         w_words = {}
 
-        def load_x(c):
-            for rt in range(ROW_TILES):
-                t = c * ROW_TILES + rt
-                raw[t] = x_pool.tile([P, TILE_GROUPS * K_PASS], BF16, name="raw")
-                nc.sync.dma_start(
-                    out=raw[t][:],
-                    in_=x_tiles[rt, :, c * TILE_GROUPS * K_PASS : (c + 1) * TILE_GROUPS * K_PASS],
-                )
+        def load_x(t):
+            c, rt = divmod(t, ROW_TILES)
+            raw[t] = x_pool.tile([P, TILE_GROUPS * K_PASS], BF16, name="raw")
+            nc.sync.dma_start(
+                out=raw[t][:],
+                in_=x_tiles[rt, :, c * TILE_GROUPS * K_PASS : (c + 1) * TILE_GROUPS * K_PASS],
+            )
 
         def load_weight_words(c):
             w_words[c] = w_pool.tile([P, TILE_GROUPS, 2, QD], U32, name="w_words", align_bytes=64)
@@ -73,15 +72,20 @@ def tile_parallelretention_pa_k_kernel(tc, x, Wk_words, Wk_scales, bk, Wv_words,
         ident_f32 = const.tile([P, P], F32, name="ident_f32")
         make_identity(nc, ident_f32[:])
 
-        load_x(0)
-        for j, dram in enumerate((Wk_scales, Wv_scales)):
-            by_row = dram.rearrange("g (quad r) n -> r quad g n", r=4)
-            for r in range(4):
-                nc.sync.dma_start(out=w_planes[r:P:32, :, j, :].bitcast(I32), in_=by_row[r].bitcast(I32))
-        load_weight_words(0)
-        for c in range(1, PREFETCH):
-            load_weight_words(c)
-            load_x(c)
+        def request(t):
+            load_x(t)
+            if t % ROW_TILES == 1:
+                if t == 1:
+                    for j, dram in enumerate((Wk_scales, Wv_scales)):
+                        by_row = dram.rearrange("g (quad r) n -> r quad g n", r=4)
+                        for r in range(4):
+                            nc.sync.dma_start(
+                                out=w_planes[r:P:32, :, j, :].bitcast(I32), in_=by_row[r].bitcast(I32)
+                            )
+                load_weight_words(t // ROW_TILES)
+
+        for t in range(PREFETCH):
+            request(t)
 
         bias_ps = banks.tile([P, 2 * QD], F32, name="bias_ps", tag="bank")
         nc.tensor.matmul(out=bias_ps[:], lhsT=ones[:], rhs=bias_rows[:], start=True, stop=True)
@@ -144,19 +148,16 @@ def tile_parallelretention_pa_k_kernel(tc, x, Wk_words, Wk_scales, bk, Wv_words,
             nc.sync.dma_start(out=out_tiles[rt], in_=product[:])
 
         for t in range(TILES):
-            c, rt = divmod(t, ROW_TILES)
-            if rt == 0 and c + PREFETCH < CHUNKS:
-                load_weight_words(c + PREFETCH)
-                load_x(c + PREFETCH)
+            if t + PREFETCH < TILES:
+                request(t + PREFETCH)
             transpose_tile(t)
             if t >= 1:
                 quantise(t - 1)
-            if t % 2 == 1:
-                if t >= 2:
-                    multiply(t - 2)
-                multiply(t - 1)
+            if t >= 2:
+                multiply(t - 2)
         finish(0)
         quantise(TILES - 1)
+        multiply(TILES - 2)
         multiply(TILES - 1)
         for rt in range(1, ROW_TILES):
             finish(rt)

@@ -33,7 +33,7 @@ def tile_parallelretention_pa_k_kernel(tc, x, Wk_words, Wk_scales, bk, Wv_words,
         const = ctx.enter_context(tc.tile_pool(name="const", bufs=1))
         x_pool = ctx.enter_context(tc.tile_pool(name="x", bufs=PREFETCH + 1))
         w_pool = ctx.enter_context(tc.tile_pool(name="w", bufs=CHUNKS))
-        stage = ctx.enter_context(tc.tile_pool(name="stage", bufs=3))
+        stage = ctx.enter_context(tc.tile_pool(name="stage", bufs=4))
         mx_pool = ctx.enter_context(tc.tile_pool(name="mx", bufs=4))
         result = ctx.enter_context(tc.tile_pool(name="result", bufs=ROW_TILES))
         banks = ctx.enter_context(tc.psum_pool(name="banks", bufs=4))
@@ -94,23 +94,26 @@ def tile_parallelretention_pa_k_kernel(tc, x, Wk_words, Wk_scales, bk, Wv_words,
 
         sums = [sums_pool.tile([P, 2 * QD], F32, name="sums%d" % rt) for rt in range(ROW_TILES)]
 
+        by_half = {}
         grouped = {}
         x_words = {}
         x_planes = {}
 
-        def transpose_tile(t):
-            by_half = stage.tile([P, TILE_GROUPS, 2, 2 * P], BF16, name="by_half")
+        def sort_pairs(t):
+            by_half[t] = stage.tile([P, TILE_GROUPS, 2, 2 * P], BF16, name="by_half")
             nc.vector.tensor_copy(
-                out=by_half[:].bitcast(F32),
+                out=by_half[t][:].bitcast(F32),
                 in_=raw[t][:].bitcast(F32).rearrange("r (g p u) -> r g u p", g=TILE_GROUPS, u=2),
             )
+
+        def transpose_tile(t):
             grouped[t] = stage.tile([P, TILE_GROUPS, P, 4], BF16, name="grouped", align_bytes=64)
             for two in range(TILE_GROUPS // 2):
                 bank = banks.tile([P, 2, 2, P], F32, name="bank")
                 for i in range(2):
                     for u in range(2):
                         nc.tensor.transpose(
-                            bank[:, i, u, :], by_half[:].bitcast(F32)[:, 2 * two + i, u, :], ident_f32[:]
+                            bank[:, i, u, :], by_half[t][:].bitcast(F32)[:, 2 * two + i, u, :], ident_f32[:]
                         )
                 nc.scalar.copy(
                     out=grouped[t][:].bitcast(F32)[:, 2 * two : 2 * two + 2, :, :],
@@ -147,9 +150,12 @@ def tile_parallelretention_pa_k_kernel(tc, x, Wk_words, Wk_scales, bk, Wv_words,
             nc.vector.tensor_mul(out=product[:], in0=biased[:, 0:QD], in1=biased[:, QD : 2 * QD])
             nc.sync.dma_start(out=out_tiles[rt], in_=product[:])
 
+        sort_pairs(0)
         for t in range(TILES):
             if t + PREFETCH < TILES:
                 request(t + PREFETCH)
+            if t + 1 < TILES:
+                sort_pairs(t + 1)
             transpose_tile(t)
             if t >= 1:
                 quantise(t - 1)

@@ -74,8 +74,8 @@ def tile_parallelretention_pa_k_kernel(tc, x, Wk_words, Wk_scales, bk, Wv_words,
 
         def request(t):
             load_x(t)
-            if t % ROW_TILES == 1:
-                if t == 1:
+            if t == 2 or (t > ROW_TILES and t % ROW_TILES == 1):
+                if t == 2:
                     for j, dram in enumerate((Wk_scales, Wv_scales)):
                         by_row = dram.rearrange("g (quad r) n -> r quad g n", r=4)
                         for r in range(4):

@@ -17,9 +17,14 @@ QD = 128
 K_PASS = 4 * P
 GROUPS = E // K_PASS
 TILE_GROUPS = 4
-CHUNKS = GROUPS // TILE_GROUPS
-TILES = CHUNKS * ROW_TILES
-PREFETCH = 12
+CHUNK_GROUPS = (4, 8, 8, 8, 4)
+CHUNK_START = tuple(sum(CHUNK_GROUPS[:c]) for c in range(len(CHUNK_GROUPS)))
+TILES = tuple(
+    (c, rt, CHUNK_START[c] + g)
+    for c in range(len(CHUNK_GROUPS))
+    for rt in range(ROW_TILES)
+    for g in range(0, CHUNK_GROUPS[c], TILE_GROUPS)
+)
 
 FLOPS = 2 * ROW_TILES * P * E * 2 * QD
 
@@ -31,8 +36,7 @@ def tile_parallelretention_pa_k_kernel(tc, x, Wk_words, Wk_scales, bk, Wv_words,
 
     with ExitStack() as ctx:
         const = ctx.enter_context(tc.tile_pool(name="const", bufs=1))
-        x_pool = ctx.enter_context(tc.tile_pool(name="x", bufs=PREFETCH + 1))
-        w_pool = ctx.enter_context(tc.tile_pool(name="w", bufs=CHUNKS))
+        loads = ctx.enter_context(tc.tile_pool(name="loads", bufs=1))
         stage = ctx.enter_context(tc.tile_pool(name="stage", bufs=4))
         mx_pool = ctx.enter_context(tc.tile_pool(name="mx", bufs=4))
         result = ctx.enter_context(tc.tile_pool(name="result", bufs=ROW_TILES))
@@ -43,22 +47,18 @@ def tile_parallelretention_pa_k_kernel(tc, x, Wk_words, Wk_scales, bk, Wv_words,
         raw = {}
         w_words = {}
 
-        def load_x(t):
-            c, rt = divmod(t, ROW_TILES)
-            raw[t] = x_pool.tile([P, TILE_GROUPS * K_PASS], BF16, name="raw")
-            nc.sync.dma_start(
-                out=raw[t][:],
-                in_=x_tiles[rt, :, c * TILE_GROUPS * K_PASS : (c + 1) * TILE_GROUPS * K_PASS],
-            )
+        def load_x(c, rt):
+            g0, n = CHUNK_START[c], CHUNK_GROUPS[c]
+            raw[c, rt] = loads.tile([P, n * K_PASS], BF16, name="raw%d_%d" % (c, rt))
+            nc.sync.dma_start(out=raw[c, rt][:], in_=x_tiles[rt, :, g0 * K_PASS : (g0 + n) * K_PASS])
 
         def load_weight_words(c):
-            w_words[c] = w_pool.tile([P, TILE_GROUPS, 2, QD], U32, name="w_words", align_bytes=64)
+            g0, n = CHUNK_START[c], CHUNK_GROUPS[c]
+            w_words[c] = loads.tile([P, n, 2, QD], U32, name="w_words%d" % c, align_bytes=64)
             for j, dram in enumerate((Wk_words, Wv_words)):
                 nc.sync.dma_start(
                     out=w_words[c][:, :, j, :].bitcast(I32),
-                    in_=dram[c * TILE_GROUPS : (c + 1) * TILE_GROUPS]
-                    .rearrange("g p n t -> p g (n t)")
-                    .bitcast(I32),
+                    in_=dram[g0 : g0 + n].rearrange("g p n t -> p g (n t)").bitcast(I32),
                 )
 
         bias_rows = const.tile([P, 2 * QD], BF16, name="bias_rows")
@@ -72,20 +72,19 @@ def tile_parallelretention_pa_k_kernel(tc, x, Wk_words, Wk_scales, bk, Wv_words,
         ident_f32 = const.tile([P, P], F32, name="ident_f32")
         make_identity(nc, ident_f32[:])
 
-        def request(t):
-            load_x(t)
-            if t == 2 or (t > ROW_TILES and t % ROW_TILES == 1):
-                if t == 2:
-                    for j, dram in enumerate((Wk_scales, Wv_scales)):
-                        by_row = dram.rearrange("g (quad r) n -> r quad g n", r=4)
-                        for r in range(4):
-                            nc.sync.dma_start(
-                                out=w_planes[r:P:32, :, j, :].bitcast(I32), in_=by_row[r].bitcast(I32)
-                            )
-                load_weight_words(t // ROW_TILES)
+        def load_scales():
+            for j, dram in enumerate((Wk_scales, Wv_scales)):
+                by_row = dram.rearrange("g (quad r) n -> r quad g n", r=4)
+                for r in range(4):
+                    nc.sync.dma_start(out=w_planes[r:P:32, :, j, :].bitcast(I32), in_=by_row[r].bitcast(I32))
 
-        for t in range(PREFETCH):
-            request(t)
+        for c in range(len(CHUNK_GROUPS)):
+            for rt in range(ROW_TILES):
+                load_x(c, rt)
+                if rt == (2 if c == 0 else 0):
+                    if c == 0:
+                        load_scales()
+                    load_weight_words(c)
 
         bias_ps = banks.tile([P, 2 * QD], F32, name="bias_ps", tag="bank")
         nc.tensor.matmul(out=bias_ps[:], lhsT=ones[:], rhs=bias_rows[:], start=True, stop=True)
@@ -100,10 +99,14 @@ def tile_parallelretention_pa_k_kernel(tc, x, Wk_words, Wk_scales, bk, Wv_words,
         x_planes = {}
 
         def sort_pairs(t):
+            c, rt, group = TILES[t]
+            k0 = (group - CHUNK_START[c]) * K_PASS
             by_half[t] = stage.tile([P, TILE_GROUPS, 2, 2 * P], BF16, name="by_half")
             nc.vector.tensor_copy(
                 out=by_half[t][:].bitcast(F32),
-                in_=raw[t][:].bitcast(F32).rearrange("r (g p u) -> r g u p", g=TILE_GROUPS, u=2),
+                in_=raw[c, rt][:, k0 : k0 + TILE_GROUPS * K_PASS]
+                .bitcast(F32)
+                .rearrange("r (g p u) -> r g u p", g=TILE_GROUPS, u=2),
             )
 
         def transpose_tile(t):
@@ -130,14 +133,14 @@ def tile_parallelretention_pa_k_kernel(tc, x, Wk_words, Wk_scales, bk, Wv_words,
             )
 
         def multiply(t):
-            c, rt = divmod(t, ROW_TILES)
+            c, rt, first = TILES[t]
             for g in range(TILE_GROUPS):
-                group = c * TILE_GROUPS + g
+                group = first + g
                 nc.tensor.matmul_mx(
                     out=sums[rt][:],
                     lhsT=x_words[t][:, g, :].bitcast(FP8X4),
                     lhsT_scale=x_planes[t][:, g, :],
-                    rhs=w_words[c][:, g].rearrange("p j n -> p (j n)").bitcast(FP8X4),
+                    rhs=w_words[c][:, group - CHUNK_START[c]].rearrange("p j n -> p (j n)").bitcast(FP8X4),
                     rhs_scale=w_planes[:, group].rearrange("p j n -> p (j n)"),
                     start=(group == 0),
                     stop=(group == GROUPS - 1),
@@ -151,10 +154,8 @@ def tile_parallelretention_pa_k_kernel(tc, x, Wk_words, Wk_scales, bk, Wv_words,
             nc.sync.dma_start(out=out_tiles[rt], in_=product[:])
 
         sort_pairs(0)
-        for t in range(TILES):
-            if t + PREFETCH < TILES:
-                request(t + PREFETCH)
-            if t + 1 < TILES:
+        for t in range(len(TILES)):
+            if t + 1 < len(TILES):
                 sort_pairs(t + 1)
             transpose_tile(t)
             if t >= 1:
@@ -162,8 +163,8 @@ def tile_parallelretention_pa_k_kernel(tc, x, Wk_words, Wk_scales, bk, Wv_words,
             if t >= 2:
                 multiply(t - 2)
         finish(0)
-        quantise(TILES - 1)
-        multiply(TILES - 2)
-        multiply(TILES - 1)
+        quantise(len(TILES) - 1)
+        multiply(len(TILES) - 2)
+        multiply(len(TILES) - 1)
         for rt in range(1, ROW_TILES):
             finish(rt)

@@ -19,12 +19,14 @@ GROUPS = E // K_PASS
 TILE_GROUPS = 4
 CHUNK_GROUPS = (4, 8, 8, 8, 4)
 CHUNK_START = tuple(sum(CHUNK_GROUPS[:c]) for c in range(len(CHUNK_GROUPS)))
+PLANES = ((0, CHUNK_GROUPS[0]), (CHUNK_GROUPS[0], GROUPS))
 TILES = tuple(
-    (c, rt, CHUNK_START[c] + g)
+    (c, rt, CHUNK_START[c] + g, TILE_GROUPS)
     for c in range(len(CHUNK_GROUPS))
     for rt in range(ROW_TILES)
     for g in range(0, CHUNK_GROUPS[c], TILE_GROUPS)
 )
+SPREAD_AT = 20
 
 FLOPS = 2 * ROW_TILES * P * E * 2 * QD
 
@@ -38,7 +40,7 @@ def tile_parallelretention_pa_k_kernel(tc, x, Wk_words, Wk_scales, bk, Wv_words,
         const = ctx.enter_context(tc.tile_pool(name="const", bufs=1))
         loads = ctx.enter_context(tc.tile_pool(name="loads", bufs=1))
         stage = ctx.enter_context(tc.tile_pool(name="stage", bufs=4))
-        mx_pool = ctx.enter_context(tc.tile_pool(name="mx", bufs=4))
+        mx_pool = ctx.enter_context(tc.tile_pool(name="mx", bufs=6))
         result = ctx.enter_context(tc.tile_pool(name="result", bufs=ROW_TILES))
         banks = ctx.enter_context(tc.psum_pool(name="banks", bufs=4))
         sums_pool = ctx.enter_context(tc.psum_pool(name="sums", bufs=1))
@@ -47,10 +49,10 @@ def tile_parallelretention_pa_k_kernel(tc, x, Wk_words, Wk_scales, bk, Wv_words,
         raw = {}
         w_words = {}
 
-        def load_x(c, rt):
+        def load_x(queue, c, rt):
             g0, n = CHUNK_START[c], CHUNK_GROUPS[c]
             raw[c, rt] = loads.tile([P, n * K_PASS], BF16, name="raw%d_%d" % (c, rt))
-            nc.sync.dma_start(out=raw[c, rt][:], in_=x_tiles[rt, :, g0 * K_PASS : (g0 + n) * K_PASS])
+            queue.dma_start(out=raw[c, rt][:], in_=x_tiles[rt, :, g0 * K_PASS : (g0 + n) * K_PASS])
 
         def load_weight_words(c):
             g0, n = CHUNK_START[c], CHUNK_GROUPS[c]
@@ -61,35 +63,40 @@ def tile_parallelretention_pa_k_kernel(tc, x, Wk_words, Wk_scales, bk, Wv_words,
                     in_=dram[g0 : g0 + n].rearrange("g p n t -> p g (n t)").bitcast(I32),
                 )
 
-        bias_rows = const.tile([P, 2 * QD], BF16, name="bias_rows")
-        nc.vector.memset(bias_rows[:], 0.0)
-        nc.scalar.dma_start(out=bias_rows[0:1, 0:QD], in_=bk.unsqueeze(0))
-        nc.scalar.dma_start(out=bias_rows[0:1, QD : 2 * QD], in_=bv.unsqueeze(0))
-        ones = const.tile([P, P], BF16, name="ones")
-        nc.vector.memset(ones[:], 1.0)
-        w_planes = const.tile([P, GROUPS, 2, QD], U8, name="w_planes", align_bytes=64)
-        nc.vector.memset(w_planes[:].rearrange("p g j n -> p (g j n)").bitcast(I32), 0)
+        load_x(nc.sync, 0, 0)
+        load_x(nc.gpsimd, 0, 1)
+        w_planes = {}
+        for g0, g1 in PLANES:
+            w_planes[g0, g1] = const.tile([P, g1 - g0, 2, QD], U8, name="w_planes%d" % g0, align_bytes=64)
+            nc.vector.memset(w_planes[g0, g1][:].rearrange("p g j n -> p (g j n)").bitcast(I32), 0)
         ident_f32 = const.tile([P, P], F32, name="ident_f32")
         make_identity(nc, ident_f32[:])
+        load_x(nc.gpsimd, 0, 2)
+        load_x(nc.gpsimd, 0, 3)
+        ones = const.tile([P, P], BF16, name="ones")
+        nc.gpsimd.memset(ones[:], 1.0)
+        bias_rows = const.tile([P, 2 * QD], BF16, name="bias_rows")
+        nc.gpsimd.memset(bias_rows[:], 0.0)
 
-        def load_scales():
+        def load_scales(g0, g1):
             for j, dram in enumerate((Wk_scales, Wv_scales)):
-                by_row = dram.rearrange("g (quad r) n -> r quad g n", r=4)
+                by_row = dram[g0:g1].rearrange("g (quad r) n -> r quad g n", r=4)
                 for r in range(4):
-                    nc.sync.dma_start(out=w_planes[r:P:32, :, j, :].bitcast(I32), in_=by_row[r].bitcast(I32))
+                    nc.sync.dma_start(
+                        out=w_planes[g0, g1][r:P:32, :, j, :].bitcast(I32), in_=by_row[r].bitcast(I32)
+                    )
 
-        for c in range(len(CHUNK_GROUPS)):
+        load_weight_words(0)
+        for g0, g1 in PLANES:
+            load_scales(g0, g1)
+        for c in range(1, len(CHUNK_GROUPS)):
             for rt in range(ROW_TILES):
-                load_x(c, rt)
-                if rt == (2 if c == 0 else 0):
-                    if c == 0:
-                        load_scales()
+                load_x(nc.sync, c, rt)
+                if rt == 1:
                     load_weight_words(c)
-
-        bias_ps = banks.tile([P, 2 * QD], F32, name="bias_ps", tag="bank")
-        nc.tensor.matmul(out=bias_ps[:], lhsT=ones[:], rhs=bias_rows[:], start=True, stop=True)
-        bias_all = const.tile([P, 2 * QD], F32, name="bias_all")
-        nc.scalar.copy(out=bias_all[:], in_=bias_ps[:])
+            if c == 1:
+                nc.sync.dma_start(out=bias_rows[0:1, 0:QD], in_=bk.unsqueeze(0))
+                nc.sync.dma_start(out=bias_rows[0:1, QD : 2 * QD], in_=bv.unsqueeze(0))
 
         sums = [sums_pool.tile([P, 2 * QD], F32, name="sums%d" % rt) for rt in range(ROW_TILES)]
 
@@ -99,72 +106,95 @@ def tile_parallelretention_pa_k_kernel(tc, x, Wk_words, Wk_scales, bk, Wv_words,
         x_planes = {}
 
         def sort_pairs(t):
-            c, rt, group = TILES[t]
+            c, rt, group, n = TILES[t]
             k0 = (group - CHUNK_START[c]) * K_PASS
-            by_half[t] = stage.tile([P, TILE_GROUPS, 2, 2 * P], BF16, name="by_half")
+            by_half[t] = stage.tile([P, n, 2, 2 * P], BF16, name="by_half")
             nc.vector.tensor_copy(
                 out=by_half[t][:].bitcast(F32),
-                in_=raw[c, rt][:, k0 : k0 + TILE_GROUPS * K_PASS]
-                .bitcast(F32)
-                .rearrange("r (g p u) -> r g u p", g=TILE_GROUPS, u=2),
+                in_=raw[c, rt][:, k0 : k0 + n * K_PASS].bitcast(F32).rearrange("r (g p u) -> r g u p", g=n, u=2),
             )
 
         def transpose_tile(t):
-            grouped[t] = stage.tile([P, TILE_GROUPS, P, 4], BF16, name="grouped", align_bytes=64)
-            for two in range(TILE_GROUPS // 2):
+            n = TILES[t][3]
+            grouped[t] = stage.tile([P, n, P, 4], BF16, name="grouped", align_bytes=64)
+            for two in range(n // 2):
                 bank = banks.tile([P, 2, 2, P], F32, name="bank")
                 for i in range(2):
                     for u in range(2):
                         nc.tensor.transpose(
                             bank[:, i, u, :], by_half[t][:].bitcast(F32)[:, 2 * two + i, u, :], ident_f32[:]
                         )
-                nc.scalar.copy(
+                copy = nc.vector.tensor_copy if (t, two) == (len(TILES) - 1, n // 2 - 1) else nc.scalar.copy
+                copy(
                     out=grouped[t][:].bitcast(F32)[:, 2 * two : 2 * two + 2, :, :],
                     in_=bank[:].rearrange("p g u r -> p g r u"),
                 )
 
         def quantise(t):
-            x_words[t] = mx_pool.tile([P, TILE_GROUPS, P], U32, name="x_words", align_bytes=64)
-            x_planes[t] = mx_pool.tile([P, TILE_GROUPS, P], U8, name="x_planes", align_bytes=64)
-            nc.vector.quantize_mx(
-                out=x_words[t][:].rearrange("p g r -> p (g r)").bitcast(FP8X4),
-                scales=x_planes[t][:].rearrange("p g r -> p (g r)"),
-                in_=grouped[t][:].rearrange("p g r t -> p (g r t)"),
-            )
+            n = TILES[t][3]
+            x_words[t] = mx_pool.tile([P, n, P], U32, name="x_words", align_bytes=64)
+            x_planes[t] = mx_pool.tile([P, n, P], U8, name="x_planes", align_bytes=64)
+            step = n // 2 if t == len(TILES) - 1 else n
+            for g in range(0, n, step):
+                nc.vector.quantize_mx(
+                    out=x_words[t][:, g : g + step].rearrange("p g r -> p (g r)").bitcast(FP8X4),
+                    scales=x_planes[t][:, g : g + step].rearrange("p g r -> p (g r)"),
+                    in_=grouped[t][:, g : g + step].rearrange("p g r t -> p (g r t)"),
+                )
 
         def multiply(t):
-            c, rt, first = TILES[t]
-            for g in range(TILE_GROUPS):
+            c, rt, first, n = TILES[t]
+            for g in range(n):
                 group = first + g
+                g0, g1 = PLANES[0 if c == 0 else 1]
                 nc.tensor.matmul_mx(
                     out=sums[rt][:],
                     lhsT=x_words[t][:, g, :].bitcast(FP8X4),
                     lhsT_scale=x_planes[t][:, g, :],
                     rhs=w_words[c][:, group - CHUNK_START[c]].rearrange("p j n -> p (j n)").bitcast(FP8X4),
-                    rhs_scale=w_planes[:, group].rearrange("p j n -> p (j n)"),
+                    rhs_scale=w_planes[g0, g1][:, group - g0].rearrange("p j n -> p (j n)"),
                     start=(group == 0),
                     stop=(group == GROUPS - 1),
                 )
 
-        def finish(rt):
-            biased = result.tile([P, 2 * QD], F32, name="biased")
-            nc.vector.tensor_add(out=biased[:], in0=sums[rt][:], in1=bias_all[:])
+        bias_all = const.tile([P, 2 * QD], F32, name="bias_all")
+
+        def spread_biases():
+            bias_ps = banks.tile([P, 2 * QD], F32, name="bias_ps", tag="bank")
+            nc.tensor.matmul(out=bias_ps[:], lhsT=ones[:], rhs=bias_rows[:], start=True, stop=True)
+            nc.scalar.copy(out=bias_all[:], in_=bias_ps[:])
+
+        biased = {}
+
+        def add_biases(rt):
+            biased[rt] = result.tile([P, 2 * QD], F32, name="biased")
+            nc.vector.tensor_add(out=biased[rt][:], in0=sums[rt][:], in1=bias_all[:])
+
+        def store_product(rt):
             product = result.tile([P, QD], F32, name="product")
-            nc.vector.tensor_mul(out=product[:], in0=biased[:, 0:QD], in1=biased[:, QD : 2 * QD])
+            nc.vector.tensor_mul(out=product[:], in0=biased[rt][:, 0:QD], in1=biased[rt][:, QD : 2 * QD])
             nc.sync.dma_start(out=out_tiles[rt], in_=product[:])
 
+        last = len(TILES) - 1
         sort_pairs(0)
-        for t in range(len(TILES)):
-            if t + 1 < len(TILES):
+        for t in range(last + 1):
+            if t < last:
                 sort_pairs(t + 1)
-            transpose_tile(t)
             if t >= 1:
                 quantise(t - 1)
+            transpose_tile(t)
+            if t == SPREAD_AT:
+                spread_biases()
             if t >= 2:
                 multiply(t - 2)
-        finish(0)
-        quantise(len(TILES) - 1)
-        multiply(len(TILES) - 2)
-        multiply(len(TILES) - 1)
-        for rt in range(1, ROW_TILES):
-            finish(rt)
+        quantise(last)
+        add_biases(0)
+        multiply(last - 1)
+        add_biases(1)
+        store_product(0)
+        multiply(last)
+        add_biases(2)
+        store_product(1)
+        store_product(2)
+        add_biases(3)
+        store_product(3)

@@ -19,7 +19,6 @@ GROUPS = E // K_PASS
 TILE_GROUPS = 4
 CHUNK_GROUPS = (4, 8, 8, 8, 4)
 CHUNK_START = tuple(sum(CHUNK_GROUPS[:c]) for c in range(len(CHUNK_GROUPS)))
-PLANES = ((0, CHUNK_GROUPS[0]), (CHUNK_GROUPS[0], GROUPS))
 TILES = tuple(
     (c, rt, CHUNK_START[c] + g, TILE_GROUPS)
     for c in range(len(CHUNK_GROUPS))
@@ -49,10 +48,15 @@ def tile_parallelretention_pa_k_kernel(tc, x, Wk_words, Wk_scales, bk, Wv_words,
         raw = {}
         w_words = {}
 
-        def load_x(queue, c, rt):
+        def load_x(c, rt):
             g0, n = CHUNK_START[c], CHUNK_GROUPS[c]
             raw[c, rt] = loads.tile([P, n * K_PASS], BF16, name="raw%d_%d" % (c, rt))
-            queue.dma_start(out=raw[c, rt][:], in_=x_tiles[rt, :, g0 * K_PASS : (g0 + n) * K_PASS])
+            step = n // 2 if (c, rt) == (len(CHUNK_GROUPS) - 1, ROW_TILES - 1) else n
+            for g in range(0, n, step):
+                nc.sync.dma_start(
+                    out=raw[c, rt][:, g * K_PASS : (g + step) * K_PASS],
+                    in_=x_tiles[rt, :, (g0 + g) * K_PASS : (g0 + g + step) * K_PASS],
+                )
 
         def load_weight_words(c):
             g0, n = CHUNK_START[c], CHUNK_GROUPS[c]
@@ -63,36 +67,27 @@ def tile_parallelretention_pa_k_kernel(tc, x, Wk_words, Wk_scales, bk, Wv_words,
                     in_=dram[g0 : g0 + n].rearrange("g p n t -> p g (n t)").bitcast(I32),
                 )
 
-        load_x(nc.sync, 0, 0)
-        load_x(nc.gpsimd, 0, 1)
-        w_planes = {}
-        for g0, g1 in PLANES:
-            w_planes[g0, g1] = const.tile([P, g1 - g0, 2, QD], U8, name="w_planes%d" % g0, align_bytes=64)
-            nc.vector.memset(w_planes[g0, g1][:].rearrange("p g j n -> p (g j n)").bitcast(I32), 0)
+        w_planes = const.tile([P, GROUPS, 2, QD], U8, name="w_planes", align_bytes=64)
+        nc.vector.memset(w_planes[:].rearrange("p g j n -> p (g j n)").bitcast(I32), 0)
+        ones = const.tile([P, 2 * QD], BF16, name="ones")
+        nc.vector.memset(ones[:], 1.0)
+        bias_rows = const.tile([P, 2 * QD], BF16, name="bias_rows")
+        nc.vector.memset(bias_rows[:], 0.0)
         ident_f32 = const.tile([P, P], F32, name="ident_f32")
         make_identity(nc, ident_f32[:])
-        load_x(nc.gpsimd, 0, 2)
-        load_x(nc.gpsimd, 0, 3)
-        ones = const.tile([P, P], BF16, name="ones")
-        nc.gpsimd.memset(ones[:], 1.0)
-        bias_rows = const.tile([P, 2 * QD], BF16, name="bias_rows")
-        nc.gpsimd.memset(bias_rows[:], 0.0)
 
-        def load_scales(g0, g1):
+        def load_scales():
             for j, dram in enumerate((Wk_scales, Wv_scales)):
-                by_row = dram[g0:g1].rearrange("g (quad r) n -> r quad g n", r=4)
+                by_row = dram.rearrange("g (quad r) n -> r quad g n", r=4)
                 for r in range(4):
-                    nc.sync.dma_start(
-                        out=w_planes[g0, g1][r:P:32, :, j, :].bitcast(I32), in_=by_row[r].bitcast(I32)
-                    )
+                    nc.sync.dma_start(out=w_planes[r:P:32, :, j, :].bitcast(I32), in_=by_row[r].bitcast(I32))
 
-        load_weight_words(0)
-        for g0, g1 in PLANES:
-            load_scales(g0, g1)
-        for c in range(1, len(CHUNK_GROUPS)):
+        for c in range(len(CHUNK_GROUPS)):
             for rt in range(ROW_TILES):
-                load_x(nc.sync, c, rt)
-                if rt == 1:
+                load_x(c, rt)
+                if rt == (2 if c == 0 else 1):
+                    if c == 0:
+                        load_scales()
                     load_weight_words(c)
             if c == 1:
                 nc.sync.dma_start(out=bias_rows[0:1, 0:QD], in_=bk.unsqueeze(0))
@@ -107,12 +102,16 @@ def tile_parallelretention_pa_k_kernel(tc, x, Wk_words, Wk_scales, bk, Wv_words,
 
         def sort_pairs(t):
             c, rt, group, n = TILES[t]
-            k0 = (group - CHUNK_START[c]) * K_PASS
+            g0 = group - CHUNK_START[c]
             by_half[t] = stage.tile([P, n, 2, 2 * P], BF16, name="by_half")
-            nc.vector.tensor_copy(
-                out=by_half[t][:].bitcast(F32),
-                in_=raw[c, rt][:, k0 : k0 + n * K_PASS].bitcast(F32).rearrange("r (g p u) -> r g u p", g=n, u=2),
-            )
+            step = n // 2 if t == len(TILES) - 1 else n
+            for g in range(0, n, step):
+                nc.vector.tensor_copy(
+                    out=by_half[t][:, g : g + step].bitcast(F32),
+                    in_=raw[c, rt][:, (g0 + g) * K_PASS : (g0 + g + step) * K_PASS]
+                    .bitcast(F32)
+                    .rearrange("r (g p u) -> r g u p", g=step, u=2),
+                )
 
         def transpose_tile(t):
             n = TILES[t][3]
@@ -146,13 +145,12 @@ def tile_parallelretention_pa_k_kernel(tc, x, Wk_words, Wk_scales, bk, Wv_words,
             c, rt, first, n = TILES[t]
             for g in range(n):
                 group = first + g
-                g0, g1 = PLANES[0 if c == 0 else 1]
                 nc.tensor.matmul_mx(
                     out=sums[rt][:],
                     lhsT=x_words[t][:, g, :].bitcast(FP8X4),
                     lhsT_scale=x_planes[t][:, g, :],
                     rhs=w_words[c][:, group - CHUNK_START[c]].rearrange("p j n -> p (j n)").bitcast(FP8X4),
-                    rhs_scale=w_planes[g0, g1][:, group - g0].rearrange("p j n -> p (j n)"),
+                    rhs_scale=w_planes[:, group].rearrange("p j n -> p (j n)"),
                     start=(group == 0),
                     stop=(group == GROUPS - 1),
                 )
@@ -161,7 +159,7 @@ def tile_parallelretention_pa_k_kernel(tc, x, Wk_words, Wk_scales, bk, Wv_words,
 
         def spread_biases():
             bias_ps = banks.tile([P, 2 * QD], F32, name="bias_ps", tag="bank")
-            nc.tensor.matmul(out=bias_ps[:], lhsT=ones[:], rhs=bias_rows[:], start=True, stop=True)
+            nc.tensor.matmul(out=bias_ps[:], lhsT=ones[:, 0:P], rhs=bias_rows[:], start=True, stop=True)
             nc.scalar.copy(out=bias_all[:], in_=bias_ps[:])
 
         biased = {}

@@ -51,12 +51,7 @@ def tile_parallelretention_pa_k_kernel(tc, x, Wk_words, Wk_scales, bk, Wv_words,
         def load_x(c, rt):
             g0, n = CHUNK_START[c], CHUNK_GROUPS[c]
             raw[c, rt] = loads.tile([P, n * K_PASS], BF16, name="raw%d_%d" % (c, rt))
-            step = n // 2 if (c, rt) == (len(CHUNK_GROUPS) - 1, ROW_TILES - 1) else n
-            for g in range(0, n, step):
-                nc.sync.dma_start(
-                    out=raw[c, rt][:, g * K_PASS : (g + step) * K_PASS],
-                    in_=x_tiles[rt, :, (g0 + g) * K_PASS : (g0 + g + step) * K_PASS],
-                )
+            nc.sync.dma_start(out=raw[c, rt][:], in_=x_tiles[rt, :, g0 * K_PASS : (g0 + n) * K_PASS])
 
         def load_weight_words(c):
             g0, n = CHUNK_START[c], CHUNK_GROUPS[c]
@@ -85,7 +80,7 @@ def tile_parallelretention_pa_k_kernel(tc, x, Wk_words, Wk_scales, bk, Wv_words,
         for c in range(len(CHUNK_GROUPS)):
             for rt in range(ROW_TILES):
                 load_x(c, rt)
-                if rt == (2 if c == 0 else 1):
+                if rt == (2 if c == 0 else 3 if c == len(CHUNK_GROUPS) - 1 else 1):
                     if c == 0:
                         load_scales()
                     load_weight_words(c)
@@ -104,14 +99,10 @@ def tile_parallelretention_pa_k_kernel(tc, x, Wk_words, Wk_scales, bk, Wv_words,
             c, rt, group, n = TILES[t]
             g0 = group - CHUNK_START[c]
             by_half[t] = stage.tile([P, n, 2, 2 * P], BF16, name="by_half")
-            step = n // 2 if t == len(TILES) - 1 else n
-            for g in range(0, n, step):
-                nc.vector.tensor_copy(
-                    out=by_half[t][:, g : g + step].bitcast(F32),
-                    in_=raw[c, rt][:, (g0 + g) * K_PASS : (g0 + g + step) * K_PASS]
-                    .bitcast(F32)
-                    .rearrange("r (g p u) -> r g u p", g=step, u=2),
-                )
+            nc.vector.tensor_copy(
+                out=by_half[t][:].bitcast(F32),
+                in_=raw[c, rt][:, g0 * K_PASS : (g0 + n) * K_PASS].bitcast(F32).rearrange("r (g p u) -> r g u p", g=n, u=2),
+            )
 
         def transpose_tile(t):
             n = TILES[t][3]

from contextlib import ExitStack

import concourse.mybir as mybir
from concourse.masks import make_identity

BF16 = mybir.dt.bfloat16
F32 = mybir.dt.float32
I32 = mybir.dt.int32
U32 = mybir.dt.uint32
U8 = mybir.dt.uint8
FP8X4 = mybir.dt.float8_e4m3fn_x4

P = 128
ROW_TILES = 4
E = 16384
QD = 128
K_PASS = 4 * P
GROUPS = E // K_PASS
TILE_GROUPS = 4
CHUNK_GROUPS = (4, 8, 8, 8, 4)
CHUNK_START = tuple(sum(CHUNK_GROUPS[:c]) for c in range(len(CHUNK_GROUPS)))
TILES = tuple(
    (c, rt, CHUNK_START[c] + g, TILE_GROUPS)
    for c in range(len(CHUNK_GROUPS))
    for rt in range(ROW_TILES)
    for g in range(0, CHUNK_GROUPS[c], TILE_GROUPS)
)
SPREAD_AT = 20

FLOPS = 2 * ROW_TILES * P * E * 2 * QD


def tile_parallelretention_pa_k_kernel(tc, x, Wk_words, Wk_scales, bk, Wv_words, Wv_scales, bv, out):
    nc = tc.nc
    x_tiles = x.rearrange("b h l e -> (b h) l e")
    out_tiles = out.rearrange("b h l n -> (b h) l n")

    with ExitStack() as ctx:
        const = ctx.enter_context(tc.tile_pool(name="const", bufs=1))
        loads = ctx.enter_context(tc.tile_pool(name="loads", bufs=1))
        stage = ctx.enter_context(tc.tile_pool(name="stage", bufs=4))
        mx_pool = ctx.enter_context(tc.tile_pool(name="mx", bufs=6))
        result = ctx.enter_context(tc.tile_pool(name="result", bufs=ROW_TILES))
        banks = ctx.enter_context(tc.psum_pool(name="banks", bufs=4))
        sums_pool = ctx.enter_context(tc.psum_pool(name="sums", bufs=1))
        ctx.enter_context(tc.manual_schedule())

        raw = {}
        w_words = {}

        def load_x(c, rt):
            g0, n = CHUNK_START[c], CHUNK_GROUPS[c]
            raw[c, rt] = loads.tile([P, n * K_PASS], BF16, name="raw%d_%d" % (c, rt))
            nc.sync.dma_start(out=raw[c, rt][:], in_=x_tiles[rt, :, g0 * K_PASS : (g0 + n) * K_PASS])

        def load_weight_words(c):
            g0, n = CHUNK_START[c], CHUNK_GROUPS[c]
            w_words[c] = loads.tile([P, n, 2, QD], U32, name="w_words%d" % c, align_bytes=64)
            for j, dram in enumerate((Wk_words, Wv_words)):
                nc.sync.dma_start(
                    out=w_words[c][:, :, j, :].bitcast(I32),
                    in_=dram[g0 : g0 + n].rearrange("g p n t -> p g (n t)").bitcast(I32),
                )

        w_planes = const.tile([P, GROUPS, 2, QD], U8, name="w_planes", align_bytes=64)
        nc.vector.memset(w_planes[:].rearrange("p g j n -> p (g j n)").bitcast(I32), 0)
        ones = const.tile([P, 2 * QD], BF16, name="ones")
        nc.vector.memset(ones[:], 1.0)
        bias_rows = const.tile([P, 2 * QD], BF16, name="bias_rows")
        nc.vector.memset(bias_rows[:], 0.0)
        ident_f32 = const.tile([P, P], F32, name="ident_f32")
        make_identity(nc, ident_f32[:])

        def load_scales():
            for j, dram in enumerate((Wk_scales, Wv_scales)):
                by_row = dram.rearrange("g (quad r) n -> r quad g n", r=4)
                for r in range(4):
                    nc.sync.dma_start(out=w_planes[r:P:32, :, j, :].bitcast(I32), in_=by_row[r].bitcast(I32))

        for c in range(len(CHUNK_GROUPS)):
            for rt in range(ROW_TILES):
                load_x(c, rt)
                if rt == (2 if c == 0 else 3 if c == len(CHUNK_GROUPS) - 1 else 1):
                    if c == 0:
                        load_scales()
                    load_weight_words(c)
            if c == 1:
                nc.sync.dma_start(out=bias_rows[0:1, 0:QD], in_=bk.unsqueeze(0))
                nc.sync.dma_start(out=bias_rows[0:1, QD : 2 * QD], in_=bv.unsqueeze(0))

        sums = [sums_pool.tile([P, 2 * QD], F32, name="sums%d" % rt) for rt in range(ROW_TILES)]

        by_half = {}
        grouped = {}
        x_words = {}
        x_planes = {}

        def sort_pairs(t):
            c, rt, group, n = TILES[t]
            g0 = group - CHUNK_START[c]
            by_half[t] = stage.tile([P, n, 2, 2 * P], BF16, name="by_half")
            nc.vector.tensor_copy(
                out=by_half[t][:].bitcast(F32),
                in_=raw[c, rt][:, g0 * K_PASS : (g0 + n) * K_PASS].bitcast(F32).rearrange("r (g p u) -> r g u p", g=n, u=2),
            )

        def transpose_tile(t):
            n = TILES[t][3]
            grouped[t] = stage.tile([P, n, P, 4], BF16, name="grouped", align_bytes=64)
            for two in range(n // 2):
                bank = banks.tile([P, 2, 2, P], F32, name="bank")
                for i in range(2):
                    for u in range(2):
                        nc.tensor.transpose(
                            bank[:, i, u, :], by_half[t][:].bitcast(F32)[:, 2 * two + i, u, :], ident_f32[:]
                        )
                copy = nc.vector.tensor_copy if (t, two) == (len(TILES) - 1, n // 2 - 1) else nc.scalar.copy
                copy(
                    out=grouped[t][:].bitcast(F32)[:, 2 * two : 2 * two + 2, :, :],
                    in_=bank[:].rearrange("p g u r -> p g r u"),
                )

        def quantise(t):
            n = TILES[t][3]
            x_words[t] = mx_pool.tile([P, n, P], U32, name="x_words", align_bytes=64)
            x_planes[t] = mx_pool.tile([P, n, P], U8, name="x_planes", align_bytes=64)
            step = n // 2 if t == len(TILES) - 1 else n
            for g in range(0, n, step):
                nc.vector.quantize_mx(
                    out=x_words[t][:, g : g + step].rearrange("p g r -> p (g r)").bitcast(FP8X4),
                    scales=x_planes[t][:, g : g + step].rearrange("p g r -> p (g r)"),
                    in_=grouped[t][:, g : g + step].rearrange("p g r t -> p (g r t)"),
                )

        def multiply(t):
            c, rt, first, n = TILES[t]
            for g in range(n):
                group = first + g
                nc.tensor.matmul_mx(
                    out=sums[rt][:],
                    lhsT=x_words[t][:, g, :].bitcast(FP8X4),
                    lhsT_scale=x_planes[t][:, g, :],
                    rhs=w_words[c][:, group - CHUNK_START[c]].rearrange("p j n -> p (j n)").bitcast(FP8X4),
                    rhs_scale=w_planes[:, group].rearrange("p j n -> p (j n)"),
                    start=(group == 0),
                    stop=(group == GROUPS - 1),
                )

        bias_all = const.tile([P, 2 * QD], F32, name="bias_all")

        def spread_biases():
            bias_ps = banks.tile([P, 2 * QD], F32, name="bias_ps", tag="bank")
            nc.tensor.matmul(out=bias_ps[:], lhsT=ones[:, 0:P], rhs=bias_rows[:], start=True, stop=True)
            nc.scalar.copy(out=bias_all[:], in_=bias_ps[:])

        biased = {}

        def add_biases(rt):
            biased[rt] = result.tile([P, 2 * QD], F32, name="biased")
            nc.vector.tensor_add(out=biased[rt][:], in0=sums[rt][:], in1=bias_all[:])

        def store_product(rt):
            product = result.tile([P, QD], F32, name="product")
            nc.vector.tensor_mul(out=product[:], in0=biased[rt][:, 0:QD], in1=biased[rt][:, QD : 2 * QD])
            nc.sync.dma_start(out=out_tiles[rt], in_=product[:])

        last = len(TILES) - 1
        sort_pairs(0)
        for t in range(last + 1):
            if t < last:
                sort_pairs(t + 1)
            if t >= 1:
                quantise(t - 1)
            transpose_tile(t)
            if t == SPREAD_AT:
                spread_biases()
            if t >= 2:
                multiply(t - 2)
        quantise(last)
        add_biases(0)
        multiply(last - 1)
        add_biases(1)
        store_product(0)
        multiply(last)
        add_biases(2)
        store_product(1)
        store_product(2)
        add_biases(3)
        store_product(3)
